import numpy as np
import ml_dtypes


def mxq(x, axis, fmt="e4m3"):
    dtype, down = {"e4m3": (ml_dtypes.float8_e4m3fn, 7), "e5m2": (ml_dtypes.float8_e5m2, 14)}[fmt]
    v = np.moveaxis(np.asarray(x, np.float32).astype(ml_dtypes.bfloat16).astype(np.float64), axis, -1)
    blocks = v.reshape(v.shape[:-1] + (-1, 32))
    amax = np.abs(blocks).max(-1, keepdims=True)
    byte = np.maximum(np.where(amax > 0, np.frexp(amax)[1] - 1 + 127, 0) - down, 1)
    scale = np.exp2(byte - 127.0)
    codes = (blocks / scale).astype(np.float32).astype(dtype).astype(np.float64)
    return np.moveaxis((codes * scale).reshape(v.shape), -1, axis)


WIDE = False


def mx_kscale(k):
    if not WIDE:
        return np.ones(k)
    levels = np.array([10, -10, 5, -5, 0])
    a = np.random.permutation(np.resize(levels, k // 512 * 4)).reshape(k // 512, 4)
    idx = np.arange(k)
    return np.exp2(a[idx // 512, idx % 128 // 32])


BF16 = ml_dtypes.bfloat16


def bf(x):
    return np.asarray(x, np.float32).astype(BF16)


def f64(x):
    return np.asarray(x).astype(np.float64)


B, DIN, H1, H2, N, I, K, O = 1024, 2048, 1024, 512, 32, 16, 256, 16
NI = N * I
LN_EPS = 1e-5


def setup_inputs():
    s, t = mx_kscale(H1), mx_kscale(H2)
    return {"h1": bf(np.maximum(np.random.standard_normal((B, H1)), 0.0) * s),
            "W2": bf(np.random.standard_normal((H1, H2)) * 1.4 / np.sqrt(H1) / s[:, None] * t),
            "b2": bf(np.random.standard_normal(H2) * 0.2 * t),
            "Wp": bf(np.random.standard_normal((N, H2, I)) * 1.4 / np.sqrt(H2) / t[None, :, None]),
            "bp": bf(np.random.standard_normal((N, I)) * 0.2),
            "ln_g": bf(1.0 + 0.1 * np.random.standard_normal((N, I))),
            "ln_b": bf(0.1 * np.random.standard_normal((N, I)))}


def reference(h1, W2, b2, Wp, bp, ln_g, ln_b):
    x = np.maximum((mxq(f64(h1), 1, "e4m3") @ mxq(f64(W2), 0, "e4m3")) + f64(b2), 0.0)
    wpf = f64(Wp).transpose(1, 0, 2).reshape(H2, NI)
    p = (mxq(x, 1, "e4m3") @ mxq(wpf, 0, "e4m3")).reshape(B, N, I) + f64(bp)
    mu = p.mean(-1, keepdims=True)
    var = ((p - mu) ** 2).mean(-1, keepdims=True)
    return (p - mu) / np.sqrt(var + LN_EPS) * f64(ln_g) + f64(ln_b)

@@ -1,0 +1,265 @@
+from contextlib import ExitStack
+
+import concourse.mybir as mybir
+from concourse.masks import make_identity
+
+F32 = mybir.dt.float32
+BF16 = mybir.dt.bfloat16
+U32 = mybir.dt.uint32
+U8 = mybir.dt.uint8
+FP8X4 = mybir.dt.float8_e4m3fn_x4
+ACT = mybir.ActivationFunctionType
+ALU = mybir.AluOpType
+
+P = 128
+PACK = 4
+K_PASS = P * PACK
+
+B, H1, H2 = 1024, 1024, 512
+CAPS, CAP_DIM = 32, 16
+NI = CAPS * CAP_DIM
+LN_EPS = 1e-5
+
+PASSES_1 = H1 // K_PASS
+H2_TILES = H2 // P
+NI_TILES = NI // P
+CAPS_PER_TILE = P // CAP_DIM
+BLOCK = 256
+ROW_TILES = BLOCK // P
+BLOCKS = B // BLOCK
+
+FLOPS = 2 * B * H1 * H2 + 2 * B * H2 * NI
+
+
+def tile_capsulenetwork_pa_kernel(tc, h1, W2, b2, Wp, bp, ln_g, ln_b, out):
+    nc = tc.nc
+    with ExitStack() as ctx:
+        keep = ctx.enter_context(tc.tile_pool(name="keep", bufs=1))
+        work = ctx.enter_context(tc.tile_pool(name="work", bufs=3))
+        psum = ctx.enter_context(tc.psum_pool(name="psum", bufs=2))
+
+        w2_raw = keep.tile([P, PASSES_1, PACK, H2], BF16)
+        for g in range(PASSES_1):
+            nc.sync.dma_start(
+                out=w2_raw[:, g].rearrange("q (u e) w -> q u (e w)", e=2),
+                in_=W2[g * K_PASS : (g + 1) * K_PASS, :].rearrange("(u q e) w -> q u (e w)", u=2, e=2),
+            )
+        h1_raw = keep.tile([P, B // P, H1], BF16)
+        wp_raw = keep.tile([P, CAPS, PACK, CAP_DIM], BF16)
+
+        def load_h1_block(blk):
+            nc.sync.dma_start(
+                out=h1_raw[:, blk * ROW_TILES : (blk + 1) * ROW_TILES, :],
+                in_=h1[blk * BLOCK : (blk + 1) * BLOCK, :].rearrange("(j p) k -> p j k", p=P),
+            )
+
+        load_h1_block(0)
+        load_h1_block(1)
+        nc.sync.dma_start(
+            out=wp_raw[:].rearrange("p n t i -> p n (t i)"),
+            in_=Wp.rearrange("n (p t) i -> p n (t i)", t=PACK),
+        )
+        load_h1_block(2)
+        load_h1_block(3)
+
+        b2_bf = keep.tile([P, H2_TILES], BF16)
+        nc.scalar.dma_start(out=b2_bf[:], in_=b2.rearrange("(m t) -> m t", t=H2_TILES))
+        vec_rows = keep.tile([P, P], BF16)
+        nc.vector.memset(vec_rows[:], 0.0)
+        for v, vec in enumerate((bp, ln_g, ln_b)):
+            nc.scalar.dma_start(
+                out=vec_rows[v * NI_TILES : (v + 1) * NI_TILES, :],
+                in_=vec.rearrange("(r n) i -> r (n i)", r=NI_TILES),
+            )
+
+        eps = keep.tile([P, 1], F32)
+        nc.vector.memset(eps[:], LN_EPS)
+        first_sqrt = keep.tile([P, 1], F32)
+        nc.scalar.activation(out=first_sqrt[:], in_=eps[:], func=ACT.Sqrt)
+
+        ident = keep.tile([P, P], F32)
+        make_identity(nc, ident[:])
+        in_capsule = keep.tile([P, CAPS_PER_TILE], F32)
+        nc.vector.tensor_reduce(
+            out=in_capsule[:],
+            in_=ident[:].rearrange("p (n i) -> p n i", i=CAP_DIM),
+            axis=mybir.AxisListType.X,
+            op=ALU.add,
+        )
+        centre = keep.tile([P, P], F32)
+        nc.vector.scalar_tensor_tensor(
+            out=centre[:].rearrange("p (n i) -> p n i", i=CAP_DIM),
+            in0=in_capsule[:].unsqueeze(2).to_broadcast([P, CAPS_PER_TILE, CAP_DIM]),
+            scalar=-1.0 / CAP_DIM,
+            in1=ident[:].rearrange("p (n i) -> p n i", i=CAP_DIM),
+            op0=ALU.mult,
+            op1=ALU.add,
+        )
+
+        b2_col = keep.tile([P, H2_TILES], F32)
+        nc.vector.tensor_copy(out=b2_col[:], in_=b2_bf[:])
+
+        vec_rows_f = keep.tile([P, P], F32)
+        nc.vector.tensor_copy(out=vec_rows_f[:], in_=vec_rows[:])
+        vec_ps = psum.tile([P, P], F32, tag="turn")
+        nc.tensor.transpose(vec_ps[:], vec_rows_f[:], ident[:])
+        vec_col = keep.tile([P, 3 * NI_TILES], F32)
+        nc.vector.tensor_copy(out=vec_col[:], in_=vec_ps[:, 0 : 3 * NI_TILES])
+        bp_col = vec_col[:, 0:NI_TILES]
+
+        def spread_over_partitions(v, name):
+            spread_ps = psum.tile([P, NI], F32, tag="centred")
+            for r in range(NI_TILES):
+                column = vec_col[:, v * NI_TILES + r : v * NI_TILES + r + 1]
+                nc.tensor.transpose(spread_ps[:, r * P : (r + 1) * P], column.to_broadcast([P, P]), ident[:])
+            spread = keep.tile([P, NI], F32, name=name)
+            nc.scalar.copy(out=spread[:], in_=spread_ps[:])
+            return spread
+
+        gain = spread_over_partitions(1, "gain")
+        shift = spread_over_partitions(2, "shift")
+
+        w2_grouped = keep.tile([P, PASSES_1, H2, PACK], BF16, align_bytes=64)
+        w2_codes = keep.tile([P, PASSES_1, H2], U32, align_bytes=64)
+        w2_scales = keep.tile([P, PASSES_1, H2], U8, align_bytes=64)
+        for g in range(PASSES_1):
+            nc.vector.tensor_copy(
+                out=w2_grouped[:, g].rearrange("p (t m) j -> p t m j", t=H2_TILES),
+                in_=w2_raw[:, g].rearrange("p j (m t) -> p t m j", t=H2_TILES),
+            )
+        for g in range(PASSES_1):
+            nc.vector.quantize_mx(
+                out=w2_codes[:, g, :].bitcast(FP8X4),
+                scales=w2_scales[:, g, :],
+                in_=w2_grouped[:, g].rearrange("p c j -> p (c j)"),
+            )
+
+        wp_grouped = keep.tile([P, CAPS, CAP_DIM, PACK], BF16, align_bytes=64)
+        wp_codes = keep.tile([P, NI], U32, align_bytes=64)
+        wp_scales = keep.tile([P, NI], U8, align_bytes=64)
+
+        def quantise_wp():
+            nc.scalar.copy(out=wp_grouped[:], in_=wp_raw[:].rearrange("p n t i -> p n i t"))
+            nc.vector.quantize_mx(
+                out=wp_codes[:].bitcast(FP8X4),
+                scales=wp_scales[:],
+                in_=wp_grouped[:].rearrange("p n i t -> p (n i t)"),
+            )
+
+        h1_words = h1_raw[:].bitcast(F32)
+        h1_grouped = keep.tile([P, BLOCKS, PASSES_1, BLOCK, PACK], BF16, align_bytes=64)
+        h1_grouped_words = h1_grouped[:].bitcast(F32)
+        h1_codes = keep.tile([P, BLOCKS, PASSES_1 * BLOCK], U32, align_bytes=64)
+        h1_scales = keep.tile([P, BLOCKS, PASSES_1 * BLOCK], U8, align_bytes=64)
+        x_tiles = keep.tile([P, H2_TILES, B], BF16)
+        x_grouped = keep.tile([P, B, PACK], BF16, align_bytes=64)
+        x_codes = keep.tile([P, B], U32, align_bytes=64)
+        x_scales = keep.tile([P, B], U8, align_bytes=64)
+        u_t = keep.tile([P, NI_TILES, B], F32)
+        out_tiles = out.rearrange("(j p) n i -> j p (n i)", p=P)
+
+        def quantise_h1(blk):
+            for jj in range(ROW_TILES):
+                j = blk * ROW_TILES + jj
+                turned = psum.tile([P, PASSES_1 * 2, P], F32, tag="turn")
+                for gu in range(PASSES_1 * 2):
+                    nc.tensor.transpose(turned[:, gu, :], h1_words[:, j, gu * P : (gu + 1) * P], ident[:])
+                nc.scalar.copy(
+                    out=h1_grouped_words[:, blk, :, jj * P : (jj + 1) * P, :],
+                    in_=turned[:].rearrange("p (g u) b -> p g b u", u=2),
+                )
+            nc.vector.quantize_mx(
+                out=h1_codes[:, blk, :].bitcast(FP8X4),
+                scales=h1_scales[:, blk, :],
+                in_=h1_grouped[:, blk].rearrange("p g b t -> p (g b t)"),
+            )
+
+        def first_product(blk):
+            rows = slice(blk * BLOCK, (blk + 1) * BLOCK)
+            for t in range(H2_TILES):
+                units = slice(t * P, (t + 1) * P)
+                acc = psum.tile([P, BLOCK], F32, tag="acc")
+                for g in range(PASSES_1):
+                    cols = slice(g * BLOCK, (g + 1) * BLOCK)
+                    nc.tensor.matmul_mx(
+                        out=acc[:],
+                        lhsT=w2_codes[:, g, units].bitcast(FP8X4),
+                        lhsT_scale=w2_scales[:, g, units],
+                        rhs=h1_codes[:, blk, cols].bitcast(FP8X4),
+                        rhs_scale=h1_scales[:, blk, cols],
+                        start=(g == 0),
+                        stop=(g == PASSES_1 - 1),
+                    )
+                nc.scalar.activation(
+                    out=x_tiles[:, t, rows], in_=acc[:], func=ACT.Relu, bias=b2_col[:, t : t + 1], scale=1.0
+                )
+            nc.vector.tensor_copy(
+                out=x_grouped[:, rows, :].rearrange("p (c i) t -> p c t i", i=4),
+                in_=x_tiles[:, :, rows].rearrange("p t (c i) -> p c t i", i=4),
+            )
+            nc.vector.quantize_mx(
+                out=x_codes[:, rows].bitcast(FP8X4),
+                scales=x_scales[:, rows],
+                in_=x_grouped[:, rows, :].rearrange("p b t -> p (b t)"),
+            )
+
+        def second_product(blk):
+            rows = slice(blk * BLOCK, (blk + 1) * BLOCK)
+            for r in range(NI_TILES):
+                cols = slice(r * P, (r + 1) * P)
+                acc_t = psum.tile([P, BLOCK], F32, tag="acc_t")
+                nc.tensor.matmul_mx(
+                    out=acc_t[:],
+                    lhsT=wp_codes[:, cols].bitcast(FP8X4),
+                    lhsT_scale=wp_scales[:, cols],
+                    rhs=x_codes[:, rows].bitcast(FP8X4),
+                    rhs_scale=x_scales[:, rows],
+                    start=True,
+                    stop=True,
+                )
+                nc.scalar.activation(
+                    out=u_t[:, r, rows], in_=acc_t[:], func=ACT.Identity, bias=bp_col[:, r : r + 1], scale=1.0
+                )
+
+        def layer_norm(j):
+            rows = slice(j * P, (j + 1) * P)
+            centred = psum.tile([P, NI], F32, tag="centred")
+            for r in range(NI_TILES):
+                nc.tensor.matmul(
+                    out=centred[:, r * P : (r + 1) * P], lhsT=u_t[:, r, rows], rhs=centre[:], start=True, stop=True
+                )
+            by_capsule = centred[:].rearrange("p (n i) -> p n i", i=CAP_DIM)
+            squares = work.tile([P, NI], F32)
+            nc.scalar.activation(out=squares[:], in_=centred[:], func=ACT.Square)
+            sum_sq = work.tile([P, CAPS], F32)
+            nc.vector.tensor_reduce(
+                out=sum_sq[:],
+                in_=squares[:].rearrange("p (n i) -> p n i", i=CAP_DIM),
+                axis=mybir.AxisListType.X,
+                op=ALU.add,
+            )
+            std = work.tile([P, CAPS], F32)
+            nc.scalar.activation(out=std[:], in_=sum_sq[:], func=ACT.Sqrt, bias=eps[:, 0:1], scale=1.0 / CAP_DIM)
+            rstd = work.tile([P, CAPS], F32)
+            nc.vector.reciprocal(out=rstd[:], in_=std[:])
+            normed = work.tile([P, NI], F32)
+            nc.vector.tensor_tensor(
+                out=normed[:].rearrange("p (n i) -> p n i", i=CAP_DIM),
+                in0=by_capsule,
+                in1=rstd[:].unsqueeze(2).to_broadcast([P, CAPS, CAP_DIM]),
+                op=ALU.mult,
+            )
+            scaled = work.tile([P, NI], F32)
+            nc.gpsimd.tensor_tensor(out=scaled[:], in0=normed[:], in1=gain[:], op=ALU.mult)
+            result = work.tile([P, NI], F32)
+            nc.vector.tensor_tensor(out=result[:], in0=scaled[:], in1=shift[:], op=ALU.add)
+            nc.sync.dma_start(out=out_tiles[j], in_=result[:])
+
+        for blk in range(BLOCKS):
+            quantise_h1(blk)
+            first_product(blk)
+            if blk == 0:
+                quantise_wp()
+            second_product(blk)
+            for jj in range(ROW_TILES):
+                layer_norm(blk * ROW_TILES + jj)

@@ -36,7 +36,17 @@ def tile_capsulenetwork_pa_kernel(tc, h1, W2, b2, Wp, bp, ln_g, ln_b, out):
     with ExitStack() as ctx:
         keep = ctx.enter_context(tc.tile_pool(name="keep", bufs=1))
         work = ctx.enter_context(tc.tile_pool(name="work", bufs=3))
-        psum = ctx.enter_context(tc.psum_pool(name="psum", bufs=2))
+        psum = ctx.enter_context(tc.psum_pool(name="psum", bufs=4))
+
+        b2_bf = keep.tile([P, H2_TILES], BF16)
+        nc.sync.dma_start(out=b2_bf[:], in_=b2.rearrange("(m t) -> m t", t=H2_TILES))
+        vec_rows = keep.tile([P, P], BF16)
+        nc.vector.memset(vec_rows[:], 0.0)
+        for v, vec in enumerate((bp, ln_g, ln_b)):
+            nc.sync.dma_start(
+                out=vec_rows[v * NI_TILES : (v + 1) * NI_TILES, :],
+                in_=vec.rearrange("(r n) i -> r (n i)", r=NI_TILES),
+            )
 
         w2_raw = keep.tile([P, PASSES_1, PACK, H2], BF16)
         for g in range(PASSES_1):
@@ -53,29 +63,17 @@ def tile_capsulenetwork_pa_kernel(tc, h1, W2, b2, Wp, bp, ln_g, ln_b, out):
                 in_=h1[blk * BLOCK : (blk + 1) * BLOCK, :].rearrange("(j p) k -> p j k", p=P),
             )
 
-        load_h1_block(0)
-        load_h1_block(1)
+        for blk in range(BLOCKS):
+            load_h1_block(blk)
         nc.sync.dma_start(
             out=wp_raw[:].rearrange("p n t i -> p n (t i)"),
             in_=Wp.rearrange("n (p t) i -> p n (t i)", t=PACK),
         )
-        load_h1_block(2)
-        load_h1_block(3)
-
-        b2_bf = keep.tile([P, H2_TILES], BF16)
-        nc.scalar.dma_start(out=b2_bf[:], in_=b2.rearrange("(m t) -> m t", t=H2_TILES))
-        vec_rows = keep.tile([P, P], BF16)
-        nc.vector.memset(vec_rows[:], 0.0)
-        for v, vec in enumerate((bp, ln_g, ln_b)):
-            nc.scalar.dma_start(
-                out=vec_rows[v * NI_TILES : (v + 1) * NI_TILES, :],
-                in_=vec.rearrange("(r n) i -> r (n i)", r=NI_TILES),
-            )
 
         eps = keep.tile([P, 1], F32)
         nc.vector.memset(eps[:], LN_EPS)
-        first_sqrt = keep.tile([P, 1], F32)
-        nc.scalar.activation(out=first_sqrt[:], in_=eps[:], func=ACT.Sqrt)
+        first_rsqrt = keep.tile([P, 1], F32)
+        nc.scalar.activation(out=first_rsqrt[:], in_=eps[:], func=ACT.Abs_reciprocal_sqrt)
 
         ident = keep.tile([P, P], F32)
         make_identity(nc, ident[:])
@@ -101,14 +99,14 @@ def tile_capsulenetwork_pa_kernel(tc, h1, W2, b2, Wp, bp, ln_g, ln_b, out):
 
         vec_rows_f = keep.tile([P, P], F32)
         nc.vector.tensor_copy(out=vec_rows_f[:], in_=vec_rows[:])
-        vec_ps = psum.tile([P, P], F32, tag="turn")
+        vec_ps = psum.tile([P, P], F32, tag="plain")
         nc.tensor.transpose(vec_ps[:], vec_rows_f[:], ident[:])
         vec_col = keep.tile([P, 3 * NI_TILES], F32)
         nc.vector.tensor_copy(out=vec_col[:], in_=vec_ps[:, 0 : 3 * NI_TILES])
         bp_col = vec_col[:, 0:NI_TILES]
 
         def spread_over_partitions(v, name):
-            spread_ps = psum.tile([P, NI], F32, tag="centred")
+            spread_ps = psum.tile([P, NI], F32, tag="plain")
             for r in range(NI_TILES):
                 column = vec_col[:, v * NI_TILES + r : v * NI_TILES + r + 1]
                 nc.tensor.transpose(spread_ps[:, r * P : (r + 1) * P], column.to_broadcast([P, P]), ident[:])
@@ -139,7 +137,7 @@ def tile_capsulenetwork_pa_kernel(tc, h1, W2, b2, Wp, bp, ln_g, ln_b, out):
         wp_scales = keep.tile([P, NI], U8, align_bytes=64)
 
         def quantise_wp():
-            nc.scalar.copy(out=wp_grouped[:], in_=wp_raw[:].rearrange("p n t i -> p n i t"))
+            nc.vector.tensor_copy(out=wp_grouped[:], in_=wp_raw[:].rearrange("p n t i -> p n i t"))
             nc.vector.quantize_mx(
                 out=wp_codes[:].bitcast(FP8X4),
                 scales=wp_scales[:],
@@ -161,7 +159,7 @@ def tile_capsulenetwork_pa_kernel(tc, h1, W2, b2, Wp, bp, ln_g, ln_b, out):
         def quantise_h1(blk):
             for jj in range(ROW_TILES):
                 j = blk * ROW_TILES + jj
-                turned = psum.tile([P, PASSES_1 * 2, P], F32, tag="turn")
+                turned = psum.tile([P, PASSES_1 * 2, P], F32, tag="plain")
                 for gu in range(PASSES_1 * 2):
                     nc.tensor.transpose(turned[:, gu, :], h1_words[:, j, gu * P : (gu + 1) * P], ident[:])
                 nc.scalar.copy(
@@ -178,7 +176,7 @@ def tile_capsulenetwork_pa_kernel(tc, h1, W2, b2, Wp, bp, ln_g, ln_b, out):
             rows = slice(blk * BLOCK, (blk + 1) * BLOCK)
             for t in range(H2_TILES):
                 units = slice(t * P, (t + 1) * P)
-                acc = psum.tile([P, BLOCK], F32, tag="acc")
+                acc = psum.tile([P, BLOCK], F32, tag="mx")
                 for g in range(PASSES_1):
                     cols = slice(g * BLOCK, (g + 1) * BLOCK)
                     nc.tensor.matmul_mx(
@@ -207,7 +205,7 @@ def tile_capsulenetwork_pa_kernel(tc, h1, W2, b2, Wp, bp, ln_g, ln_b, out):
             rows = slice(blk * BLOCK, (blk + 1) * BLOCK)
             for r in range(NI_TILES):
                 cols = slice(r * P, (r + 1) * P)
-                acc_t = psum.tile([P, BLOCK], F32, tag="acc_t")
+                acc_t = psum.tile([P, BLOCK], F32, tag="mx")
                 nc.tensor.matmul_mx(
                     out=acc_t[:],
                     lhsT=wp_codes[:, cols].bitcast(FP8X4),
@@ -223,7 +221,7 @@ def tile_capsulenetwork_pa_kernel(tc, h1, W2, b2, Wp, bp, ln_g, ln_b, out):
 
         def layer_norm(j):
             rows = slice(j * P, (j + 1) * P)
-            centred = psum.tile([P, NI], F32, tag="centred")
+            centred = psum.tile([P, NI], F32, tag="plain")
             for r in range(NI_TILES):
                 nc.tensor.matmul(
                     out=centred[:, r * P : (r + 1) * P], lhsT=u_t[:, r, rows], rhs=centre[:], start=True, stop=True
@@ -238,10 +236,10 @@ def tile_capsulenetwork_pa_kernel(tc, h1, W2, b2, Wp, bp, ln_g, ln_b, out):
                 axis=mybir.AxisListType.X,
                 op=ALU.add,
             )
-            std = work.tile([P, CAPS], F32)
-            nc.scalar.activation(out=std[:], in_=sum_sq[:], func=ACT.Sqrt, bias=eps[:, 0:1], scale=1.0 / CAP_DIM)
             rstd = work.tile([P, CAPS], F32)
-            nc.vector.reciprocal(out=rstd[:], in_=std[:])
+            nc.scalar.activation(
+                out=rstd[:], in_=sum_sq[:], func=ACT.Abs_reciprocal_sqrt, bias=eps[:, 0:1], scale=1.0 / CAP_DIM
+            )
             normed = work.tile([P, NI], F32)
             nc.vector.tensor_tensor(
                 out=normed[:].rearrange("p (n i) -> p n i", i=CAP_DIM),
@@ -257,9 +255,13 @@ def tile_capsulenetwork_pa_kernel(tc, h1, W2, b2, Wp, bp, ln_g, ln_b, out):
 
         for blk in range(BLOCKS):
             quantise_h1(blk)
+        quantise_wp()
+        for blk in range(BLOCKS):
             first_product(blk)
-            if blk == 0:
-                quantise_wp()
-            second_product(blk)
+
+        second_product(0)
+        for blk in range(BLOCKS):
+            if blk + 1 < BLOCKS:
+                second_product(blk + 1)
             for jj in range(ROW_TILES):
                 layer_norm(blk * ROW_TILES + jj)

@@ -27,6 +27,8 @@ CAPS_PER_TILE = P // CAP_DIM
 BLOCK = 256
 ROW_TILES = BLOCK // P
 BLOCKS = B // BLOCK
+LAST_ROW_TILE = B // P - 1
+W2_VECTOR_UNITS = 96
 
 FLOPS = 2 * B * H1 * H2 + 2 * B * H2 * NI
 
@@ -38,24 +40,15 @@ def tile_capsulenetwork_pa_kernel(tc, h1, W2, b2, Wp, bp, ln_g, ln_b, out):
         work = ctx.enter_context(tc.tile_pool(name="work", bufs=3))
         psum = ctx.enter_context(tc.psum_pool(name="psum", bufs=4))
 
-        b2_bf = keep.tile([P, H2_TILES], BF16)
-        nc.sync.dma_start(out=b2_bf[:], in_=b2.rearrange("(m t) -> m t", t=H2_TILES))
-        vec_rows = keep.tile([P, P], BF16)
-        nc.vector.memset(vec_rows[:], 0.0)
-        for v, vec in enumerate((bp, ln_g, ln_b)):
-            nc.sync.dma_start(
-                out=vec_rows[v * NI_TILES : (v + 1) * NI_TILES, :],
-                in_=vec.rearrange("(r n) i -> r (n i)", r=NI_TILES),
-            )
-
         w2_raw = keep.tile([P, PASSES_1, PACK, H2], BF16)
-        for g in range(PASSES_1):
+        h1_raw = keep.tile([P, B // P, H1], BF16)
+        wp_raw = keep.tile([P, CAPS, PACK, CAP_DIM], BF16)
+
+        def load_w2_pass(g):
             nc.sync.dma_start(
                 out=w2_raw[:, g].rearrange("q (u e) w -> q u (e w)", e=2),
                 in_=W2[g * K_PASS : (g + 1) * K_PASS, :].rearrange("(u q e) w -> q u (e w)", u=2, e=2),
             )
-        h1_raw = keep.tile([P, B // P, H1], BF16)
-        wp_raw = keep.tile([P, CAPS, PACK, CAP_DIM], BF16)
 
         def load_h1_block(blk):
             nc.sync.dma_start(
@@ -63,12 +56,25 @@ def tile_capsulenetwork_pa_kernel(tc, h1, W2, b2, Wp, bp, ln_g, ln_b, out):
                 in_=h1[blk * BLOCK : (blk + 1) * BLOCK, :].rearrange("(j p) k -> p j k", p=P),
             )
 
-        for blk in range(BLOCKS):
+        load_w2_pass(0)
+        load_h1_block(0)
+        load_w2_pass(1)
+        for blk in range(1, BLOCKS):
             load_h1_block(blk)
         nc.sync.dma_start(
             out=wp_raw[:].rearrange("p n t i -> p n (t i)"),
             in_=Wp.rearrange("n (p t) i -> p n (t i)", t=PACK),
         )
+
+        b2_bf = keep.tile([P, H2_TILES], BF16)
+        nc.scalar.dma_start(out=b2_bf[:], in_=b2.rearrange("(m t) -> m t", t=H2_TILES))
+        vec_rows = keep.tile([P, P], BF16)
+        nc.vector.memset(vec_rows[:], 0.0)
+        for v, vec in enumerate((bp, ln_g, ln_b)):
+            nc.scalar.dma_start(
+                out=vec_rows[v * NI_TILES : (v + 1) * NI_TILES, :],
+                in_=vec.rearrange("(r n) i -> r (n i)", r=NI_TILES),
+            )
 
         eps = keep.tile([P, 1], F32)
         nc.vector.memset(eps[:], LN_EPS)
@@ -97,34 +103,14 @@ def tile_capsulenetwork_pa_kernel(tc, h1, W2, b2, Wp, bp, ln_g, ln_b, out):
         b2_col = keep.tile([P, H2_TILES], F32)
         nc.vector.tensor_copy(out=b2_col[:], in_=b2_bf[:])
 
-        vec_rows_f = keep.tile([P, P], F32)
-        nc.vector.tensor_copy(out=vec_rows_f[:], in_=vec_rows[:])
-        vec_ps = psum.tile([P, P], F32, tag="plain")
-        nc.tensor.transpose(vec_ps[:], vec_rows_f[:], ident[:])
-        vec_col = keep.tile([P, 3 * NI_TILES], F32)
-        nc.vector.tensor_copy(out=vec_col[:], in_=vec_ps[:, 0 : 3 * NI_TILES])
-        bp_col = vec_col[:, 0:NI_TILES]
-
-        def spread_over_partitions(v, name):
-            spread_ps = psum.tile([P, NI], F32, tag="plain")
-            for r in range(NI_TILES):
-                column = vec_col[:, v * NI_TILES + r : v * NI_TILES + r + 1]
-                nc.tensor.transpose(spread_ps[:, r * P : (r + 1) * P], column.to_broadcast([P, P]), ident[:])
-            spread = keep.tile([P, NI], F32, name=name)
-            nc.scalar.copy(out=spread[:], in_=spread_ps[:])
-            return spread
-
-        gain = spread_over_partitions(1, "gain")
-        shift = spread_over_partitions(2, "shift")
-
         w2_grouped = keep.tile([P, PASSES_1, H2, PACK], BF16, align_bytes=64)
         w2_codes = keep.tile([P, PASSES_1, H2], U32, align_bytes=64)
         w2_scales = keep.tile([P, PASSES_1, H2], U8, align_bytes=64)
         for g in range(PASSES_1):
-            nc.vector.tensor_copy(
-                out=w2_grouped[:, g].rearrange("p (t m) j -> p t m j", t=H2_TILES),
-                in_=w2_raw[:, g].rearrange("p j (m t) -> p t m j", t=H2_TILES),
-            )
+            grouped = w2_grouped[:, g].rearrange("p (t m) j -> p t m j", t=H2_TILES)
+            raw = w2_raw[:, g].rearrange("p j (m t) -> p t m j", t=H2_TILES)
+            nc.vector.tensor_copy(out=grouped[:, :, 0:W2_VECTOR_UNITS, :], in_=raw[:, :, 0:W2_VECTOR_UNITS, :])
+            nc.scalar.copy(out=grouped[:, :, W2_VECTOR_UNITS:P, :], in_=raw[:, :, W2_VECTOR_UNITS:P, :])
         for g in range(PASSES_1):
             nc.vector.quantize_mx(
                 out=w2_codes[:, g, :].bitcast(FP8X4),
@@ -226,7 +212,6 @@ def tile_capsulenetwork_pa_kernel(tc, h1, W2, b2, Wp, bp, ln_g, ln_b, out):
                 nc.tensor.matmul(
                     out=centred[:, r * P : (r + 1) * P], lhsT=u_t[:, r, rows], rhs=centre[:], start=True, stop=True
                 )
-            by_capsule = centred[:].rearrange("p (n i) -> p n i", i=CAP_DIM)
             squares = work.tile([P, NI], F32)
             nc.scalar.activation(out=squares[:], in_=centred[:], func=ACT.Square)
             sum_sq = work.tile([P, CAPS], F32)
@@ -240,15 +225,16 @@ def tile_capsulenetwork_pa_kernel(tc, h1, W2, b2, Wp, bp, ln_g, ln_b, out):
             nc.scalar.activation(
                 out=rstd[:], in_=sum_sq[:], func=ACT.Abs_reciprocal_sqrt, bias=eps[:, 0:1], scale=1.0 / CAP_DIM
             )
-            normed = work.tile([P, NI], F32)
-            nc.vector.tensor_tensor(
-                out=normed[:].rearrange("p (n i) -> p n i", i=CAP_DIM),
-                in0=by_capsule,
+            factor = work.tile([P, NI], F32)
+            factor_engine = nc.vector if j == LAST_ROW_TILE else nc.gpsimd
+            factor_engine.tensor_tensor(
+                out=factor[:].rearrange("p (n i) -> p n i", i=CAP_DIM),
+                in0=gain[:].rearrange("p (n i) -> p n i", i=CAP_DIM),
                 in1=rstd[:].unsqueeze(2).to_broadcast([P, CAPS, CAP_DIM]),
                 op=ALU.mult,
             )
             scaled = work.tile([P, NI], F32)
-            nc.gpsimd.tensor_tensor(out=scaled[:], in0=normed[:], in1=gain[:], op=ALU.mult)
+            nc.vector.tensor_tensor(out=scaled[:], in0=centred[:], in1=factor[:], op=ALU.mult)
             result = work.tile([P, NI], F32)
             nc.vector.tensor_tensor(out=result[:], in0=scaled[:], in1=shift[:], op=ALU.add)
             nc.sync.dma_start(out=out_tiles[j], in_=result[:])
@@ -258,6 +244,26 @@ def tile_capsulenetwork_pa_kernel(tc, h1, W2, b2, Wp, bp, ln_g, ln_b, out):
         quantise_wp()
         for blk in range(BLOCKS):
             first_product(blk)
+
+        vec_rows_f = keep.tile([P, P], F32)
+        nc.vector.tensor_copy(out=vec_rows_f[:], in_=vec_rows[:])
+        vec_ps = psum.tile([P, P], F32, tag="plain")
+        nc.tensor.transpose(vec_ps[:], vec_rows_f[:], ident[:])
+        vec_col = keep.tile([P, 3 * NI_TILES], F32)
+        nc.vector.tensor_copy(out=vec_col[:], in_=vec_ps[:, 0 : 3 * NI_TILES])
+        bp_col = vec_col[:, 0:NI_TILES]
+
+        def spread_over_partitions(v, name):
+            spread_ps = psum.tile([P, NI], F32, tag="plain")
+            for r in range(NI_TILES):
+                column = vec_col[:, v * NI_TILES + r : v * NI_TILES + r + 1]
+                nc.tensor.transpose(spread_ps[:, r * P : (r + 1) * P], column.to_broadcast([P, P]), ident[:])
+            spread = keep.tile([P, NI], F32, name=name)
+            nc.scalar.copy(out=spread[:], in_=spread_ps[:])
+            return spread
+
+        gain = spread_over_partitions(1, "gain")
+        shift = spread_over_partitions(2, "shift")
 
         second_product(0)
         for blk in range(BLOCKS):

@@ -24,10 +24,8 @@ PASSES_1 = H1 // K_PASS
 H2_TILES = H2 // P
 NI_TILES = NI // P
 CAPS_PER_TILE = P // CAP_DIM
-BLOCK = 256
-ROW_TILES = BLOCK // P
-BLOCKS = B // BLOCK
-LAST_ROW_TILE = B // P - 1
+ROW_TILES = B // P
+LAST_ROW_TILE = ROW_TILES - 1
 W2_VECTOR_UNITS = 96
 
 FLOPS = 2 * B * H1 * H2 + 2 * B * H2 * NI
@@ -41,7 +39,7 @@ def tile_capsulenetwork_pa_kernel(tc, h1, W2, b2, Wp, bp, ln_g, ln_b, out):
         psum = ctx.enter_context(tc.psum_pool(name="psum", bufs=4))
 
         w2_raw = keep.tile([P, PASSES_1, PACK, H2], BF16)
-        h1_raw = keep.tile([P, B // P, H1], BF16)
+        h1_raw = keep.tile([P, ROW_TILES, H1], BF16)
         wp_raw = keep.tile([P, CAPS, PACK, CAP_DIM], BF16)
 
         def load_w2_pass(g):
@@ -50,31 +48,28 @@ def tile_capsulenetwork_pa_kernel(tc, h1, W2, b2, Wp, bp, ln_g, ln_b, out):
                 in_=W2[g * K_PASS : (g + 1) * K_PASS, :].rearrange("(u q e) w -> q u (e w)", u=2, e=2),
             )
 
-        def load_h1_block(blk):
-            nc.sync.dma_start(
-                out=h1_raw[:, blk * ROW_TILES : (blk + 1) * ROW_TILES, :],
-                in_=h1[blk * BLOCK : (blk + 1) * BLOCK, :].rearrange("(j p) k -> p j k", p=P),
-            )
+        def load_h1_tile(j):
+            nc.sync.dma_start(out=h1_raw[:, j, :], in_=h1[j * P : (j + 1) * P, :])
 
         load_w2_pass(0)
-        load_h1_block(0)
+        load_h1_tile(0)
         load_w2_pass(1)
-        for blk in range(1, BLOCKS):
-            load_h1_block(blk)
+        for j in range(1, ROW_TILES):
+            load_h1_tile(j)
         nc.sync.dma_start(
             out=wp_raw[:].rearrange("p n t i -> p n (t i)"),
             in_=Wp.rearrange("n (p t) i -> p n (t i)", t=PACK),
         )
+        gain = keep.tile([P, NI], BF16)
+        nc.sync.dma_start(out=gain[:], in_=ln_g.rearrange("n i -> (n i)").partition_broadcast(P))
+        shift = keep.tile([P, NI], BF16)
+        nc.sync.dma_start(out=shift[:], in_=ln_b.rearrange("n i -> (n i)").partition_broadcast(P))
 
         b2_bf = keep.tile([P, H2_TILES], BF16)
         nc.scalar.dma_start(out=b2_bf[:], in_=b2.rearrange("(m t) -> m t", t=H2_TILES))
-        vec_rows = keep.tile([P, P], BF16)
-        nc.vector.memset(vec_rows[:], 0.0)
-        for v, vec in enumerate((bp, ln_g, ln_b)):
-            nc.scalar.dma_start(
-                out=vec_rows[v * NI_TILES : (v + 1) * NI_TILES, :],
-                in_=vec.rearrange("(r n) i -> r (n i)", r=NI_TILES),
-            )
+        bp_rows = keep.tile([P, P], BF16)
+        nc.vector.memset(bp_rows[:], 0.0)
+        nc.scalar.dma_start(out=bp_rows[0:NI_TILES, :], in_=bp.rearrange("(r n) i -> r (n i)", r=NI_TILES))
 
         eps = keep.tile([P, 1], F32)
         nc.vector.memset(eps[:], LN_EPS)
@@ -131,10 +126,10 @@ def tile_capsulenetwork_pa_kernel(tc, h1, W2, b2, Wp, bp, ln_g, ln_b, out):
             )
 
         h1_words = h1_raw[:].bitcast(F32)
-        h1_grouped = keep.tile([P, BLOCKS, PASSES_1, BLOCK, PACK], BF16, align_bytes=64)
+        h1_grouped = keep.tile([P, ROW_TILES, PASSES_1, P, PACK], BF16, align_bytes=64)
         h1_grouped_words = h1_grouped[:].bitcast(F32)
-        h1_codes = keep.tile([P, BLOCKS, PASSES_1 * BLOCK], U32, align_bytes=64)
-        h1_scales = keep.tile([P, BLOCKS, PASSES_1 * BLOCK], U8, align_bytes=64)
+        h1_codes = keep.tile([P, ROW_TILES, PASSES_1, P], U32, align_bytes=64)
+        h1_scales = keep.tile([P, ROW_TILES, PASSES_1, P], U8, align_bytes=64)
         x_tiles = keep.tile([P, H2_TILES, B], BF16)
         x_grouped = keep.tile([P, B, PACK], BF16, align_bytes=64)
         x_codes = keep.tile([P, B], U32, align_bytes=64)
@@ -142,40 +137,35 @@ def tile_capsulenetwork_pa_kernel(tc, h1, W2, b2, Wp, bp, ln_g, ln_b, out):
         u_t = keep.tile([P, NI_TILES, B], F32)
         out_tiles = out.rearrange("(j p) n i -> j p (n i)", p=P)
 
-        def quantise_h1(blk):
-            for jj in range(ROW_TILES):
-                j = blk * ROW_TILES + jj
-                turned = psum.tile([P, PASSES_1 * 2, P], F32, tag="plain")
-                for gu in range(PASSES_1 * 2):
-                    nc.tensor.transpose(turned[:, gu, :], h1_words[:, j, gu * P : (gu + 1) * P], ident[:])
-                nc.scalar.copy(
-                    out=h1_grouped_words[:, blk, :, jj * P : (jj + 1) * P, :],
-                    in_=turned[:].rearrange("p (g u) b -> p g b u", u=2),
-                )
+        def quantise_h1(j):
+            turned = psum.tile([P, PASSES_1 * 2, P], F32, tag="plain")
+            for gu in range(PASSES_1 * 2):
+                nc.tensor.transpose(turned[:, gu, :], h1_words[:, j, gu * P : (gu + 1) * P], ident[:])
+            nc.scalar.copy(out=h1_grouped_words[:, j], in_=turned[:].rearrange("p (g u) b -> p g b u", u=2))
             nc.vector.quantize_mx(
-                out=h1_codes[:, blk, :].bitcast(FP8X4),
-                scales=h1_scales[:, blk, :],
-                in_=h1_grouped[:, blk].rearrange("p g b t -> p (g b t)"),
+                out=h1_codes[:, j].rearrange("p g b -> p (g b)").bitcast(FP8X4),
+                scales=h1_scales[:, j].rearrange("p g b -> p (g b)"),
+                in_=h1_grouped[:, j].rearrange("p g b t -> p (g b t)"),
             )
 
-        def first_product(blk):
-            rows = slice(blk * BLOCK, (blk + 1) * BLOCK)
+        def first_product(j):
+            rows = slice(j * P, (j + 1) * P)
+            acc = psum.tile([P, H2_TILES, P], F32, tag="mx")
             for t in range(H2_TILES):
                 units = slice(t * P, (t + 1) * P)
-                acc = psum.tile([P, BLOCK], F32, tag="mx")
                 for g in range(PASSES_1):
-                    cols = slice(g * BLOCK, (g + 1) * BLOCK)
                     nc.tensor.matmul_mx(
-                        out=acc[:],
+                        out=acc[:, t, :],
                         lhsT=w2_codes[:, g, units].bitcast(FP8X4),
                         lhsT_scale=w2_scales[:, g, units],
-                        rhs=h1_codes[:, blk, cols].bitcast(FP8X4),
-                        rhs_scale=h1_scales[:, blk, cols],
+                        rhs=h1_codes[:, j, g, :].bitcast(FP8X4),
+                        rhs_scale=h1_scales[:, j, g, :],
                         start=(g == 0),
                         stop=(g == PASSES_1 - 1),
                     )
+            for t in range(H2_TILES):
                 nc.scalar.activation(
-                    out=x_tiles[:, t, rows], in_=acc[:], func=ACT.Relu, bias=b2_col[:, t : t + 1], scale=1.0
+                    out=x_tiles[:, t, rows], in_=acc[:, t, :], func=ACT.Relu, bias=b2_col[:, t : t + 1], scale=1.0
                 )
             nc.vector.tensor_copy(
                 out=x_grouped[:, rows, :].rearrange("p (c i) t -> p c t i", i=4),
@@ -187,13 +177,13 @@ def tile_capsulenetwork_pa_kernel(tc, h1, W2, b2, Wp, bp, ln_g, ln_b, out):
                 in_=x_grouped[:, rows, :].rearrange("p b t -> p (b t)"),
             )
 
-        def second_product(blk):
-            rows = slice(blk * BLOCK, (blk + 1) * BLOCK)
+        def second_product(j):
+            rows = slice(j * P, (j + 1) * P)
+            acc_t = psum.tile([P, NI_TILES, P], F32, tag="mx")
             for r in range(NI_TILES):
                 cols = slice(r * P, (r + 1) * P)
-                acc_t = psum.tile([P, BLOCK], F32, tag="mx")
                 nc.tensor.matmul_mx(
-                    out=acc_t[:],
+                    out=acc_t[:, r, :],
                     lhsT=wp_codes[:, cols].bitcast(FP8X4),
                     lhsT_scale=wp_scales[:, cols],
                     rhs=x_codes[:, rows].bitcast(FP8X4),
@@ -201,8 +191,9 @@ def tile_capsulenetwork_pa_kernel(tc, h1, W2, b2, Wp, bp, ln_g, ln_b, out):
                     start=True,
                     stop=True,
                 )
+            for r in range(NI_TILES):
                 nc.scalar.activation(
-                    out=u_t[:, r, rows], in_=acc_t[:], func=ACT.Identity, bias=bp_col[:, r : r + 1], scale=1.0
+                    out=u_t[:, r, rows], in_=acc_t[:, r, :], func=ACT.Identity, bias=bp_col[:, r : r + 1], scale=1.0
                 )
 
         def layer_norm(j):
@@ -239,35 +230,21 @@ def tile_capsulenetwork_pa_kernel(tc, h1, W2, b2, Wp, bp, ln_g, ln_b, out):
             nc.vector.tensor_tensor(out=result[:], in0=scaled[:], in1=shift[:], op=ALU.add)
             nc.sync.dma_start(out=out_tiles[j], in_=result[:])
 
-        for blk in range(BLOCKS):
-            quantise_h1(blk)
+        for j in range(ROW_TILES):
+            quantise_h1(j)
         quantise_wp()
-        for blk in range(BLOCKS):
-            first_product(blk)
+        for j in range(ROW_TILES):
+            first_product(j)
 
-        vec_rows_f = keep.tile([P, P], F32)
-        nc.vector.tensor_copy(out=vec_rows_f[:], in_=vec_rows[:])
-        vec_ps = psum.tile([P, P], F32, tag="plain")
-        nc.tensor.transpose(vec_ps[:], vec_rows_f[:], ident[:])
-        vec_col = keep.tile([P, 3 * NI_TILES], F32)
-        nc.vector.tensor_copy(out=vec_col[:], in_=vec_ps[:, 0 : 3 * NI_TILES])
-        bp_col = vec_col[:, 0:NI_TILES]
-
-        def spread_over_partitions(v, name):
-            spread_ps = psum.tile([P, NI], F32, tag="plain")
-            for r in range(NI_TILES):
-                column = vec_col[:, v * NI_TILES + r : v * NI_TILES + r + 1]
-                nc.tensor.transpose(spread_ps[:, r * P : (r + 1) * P], column.to_broadcast([P, P]), ident[:])
-            spread = keep.tile([P, NI], F32, name=name)
-            nc.scalar.copy(out=spread[:], in_=spread_ps[:])
-            return spread
-
-        gain = spread_over_partitions(1, "gain")
-        shift = spread_over_partitions(2, "shift")
+        bp_rows_f = keep.tile([P, P], F32)
+        nc.vector.tensor_copy(out=bp_rows_f[:], in_=bp_rows[:])
+        bp_ps = psum.tile([P, P], F32, tag="plain")
+        nc.tensor.transpose(bp_ps[:], bp_rows_f[:], ident[:])
+        bp_col = keep.tile([P, NI_TILES], F32)
+        nc.vector.tensor_copy(out=bp_col[:], in_=bp_ps[:, 0:NI_TILES])
 
         second_product(0)
-        for blk in range(BLOCKS):
-            if blk + 1 < BLOCKS:
-                second_product(blk + 1)
-            for jj in range(ROW_TILES):
-                layer_norm(blk * ROW_TILES + jj)
+        for j in range(ROW_TILES):
+            if j + 1 < ROW_TILES:
+                second_product(j + 1)
+            layer_norm(j)

@@ -216,9 +216,10 @@ def tile_capsulenetwork_pa_kernel(tc, h1, W2, b2, Wp, bp, ln_g, ln_b, out):
             nc.scalar.activation(
                 out=rstd[:], in_=sum_sq[:], func=ACT.Abs_reciprocal_sqrt, bias=eps[:, 0:1], scale=1.0 / CAP_DIM
             )
+            helper = nc.vector if j == LAST_ROW_TILE else nc.gpsimd
+            adder = helper if j % 2 == 1 else nc.vector
             factor = work.tile([P, NI], F32)
-            factor_engine = nc.vector if j == LAST_ROW_TILE else nc.gpsimd
-            factor_engine.tensor_tensor(
+            helper.tensor_tensor(
                 out=factor[:].rearrange("p (n i) -> p n i", i=CAP_DIM),
                 in0=gain[:].rearrange("p (n i) -> p n i", i=CAP_DIM),
                 in1=rstd[:].unsqueeze(2).to_broadcast([P, CAPS, CAP_DIM]),
@@ -227,7 +228,7 @@ def tile_capsulenetwork_pa_kernel(tc, h1, W2, b2, Wp, bp, ln_g, ln_b, out):
             scaled = work.tile([P, NI], F32)
             nc.vector.tensor_tensor(out=scaled[:], in0=centred[:], in1=factor[:], op=ALU.mult)
             result = work.tile([P, NI], F32)
-            nc.vector.tensor_tensor(out=result[:], in0=scaled[:], in1=shift[:], op=ALU.add)
+            adder.tensor_tensor(out=result[:], in0=scaled[:], in1=shift[:], op=ALU.add)
             nc.sync.dma_start(out=out_tiles[j], in_=result[:])
 
         for j in range(ROW_TILES):

@@ -36,7 +36,8 @@ def tile_capsulenetwork_pa_kernel(tc, h1, W2, b2, Wp, bp, ln_g, ln_b, out):
     with ExitStack() as ctx:
         keep = ctx.enter_context(tc.tile_pool(name="keep", bufs=1))
         work = ctx.enter_context(tc.tile_pool(name="work", bufs=3))
-        psum = ctx.enter_context(tc.psum_pool(name="psum", bufs=4))
+        psum = ctx.enter_context(tc.psum_pool(name="psum", bufs=6))
+        psum_mx = ctx.enter_context(tc.psum_pool(name="psum_mx", bufs=2))
 
         w2_raw = keep.tile([P, PASSES_1, PACK, H2], BF16)
         h1_raw = keep.tile([P, ROW_TILES, H1], BF16)
@@ -150,7 +151,7 @@ def tile_capsulenetwork_pa_kernel(tc, h1, W2, b2, Wp, bp, ln_g, ln_b, out):
 
         def first_product(j):
             rows = slice(j * P, (j + 1) * P)
-            acc = psum.tile([P, H2_TILES, P], F32, tag="mx")
+            acc = psum_mx.tile([P, H2_TILES, P], F32, tag="mx")
             for t in range(H2_TILES):
                 units = slice(t * P, (t + 1) * P)
                 for g in range(PASSES_1):
@@ -179,7 +180,7 @@ def tile_capsulenetwork_pa_kernel(tc, h1, W2, b2, Wp, bp, ln_g, ln_b, out):
 
         def second_product(j):
             rows = slice(j * P, (j + 1) * P)
-            acc_t = psum.tile([P, NI_TILES, P], F32, tag="mx")
+            acc_t = psum_mx.tile([P, NI_TILES, P], F32, tag="mx")
             for r in range(NI_TILES):
                 cols = slice(r * P, (r + 1) * P)
                 nc.tensor.matmul_mx(
@@ -216,10 +217,9 @@ def tile_capsulenetwork_pa_kernel(tc, h1, W2, b2, Wp, bp, ln_g, ln_b, out):
             nc.scalar.activation(
                 out=rstd[:], in_=sum_sq[:], func=ACT.Abs_reciprocal_sqrt, bias=eps[:, 0:1], scale=1.0 / CAP_DIM
             )
-            helper = nc.vector if j == LAST_ROW_TILE else nc.gpsimd
-            adder = helper if j % 2 == 1 else nc.vector
             factor = work.tile([P, NI], F32)
-            helper.tensor_tensor(
+            factor_engine = nc.vector if j == LAST_ROW_TILE else nc.gpsimd
+            factor_engine.tensor_tensor(
                 out=factor[:].rearrange("p (n i) -> p n i", i=CAP_DIM),
                 in0=gain[:].rearrange("p (n i) -> p n i", i=CAP_DIM),
                 in1=rstd[:].unsqueeze(2).to_broadcast([P, CAPS, CAP_DIM]),
@@ -228,7 +228,7 @@ def tile_capsulenetwork_pa_kernel(tc, h1, W2, b2, Wp, bp, ln_g, ln_b, out):
             scaled = work.tile([P, NI], F32)
             nc.vector.tensor_tensor(out=scaled[:], in0=centred[:], in1=factor[:], op=ALU.mult)
             result = work.tile([P, NI], F32)
-            adder.tensor_tensor(out=result[:], in0=scaled[:], in1=shift[:], op=ALU.add)
+            nc.vector.tensor_tensor(out=result[:], in0=scaled[:], in1=shift[:], op=ALU.add)
             nc.sync.dma_start(out=out_tiles[j], in_=result[:])
 
         for j in range(ROW_TILES):

from contextlib import ExitStack

import concourse.mybir as mybir
from concourse.masks import make_identity

F32 = mybir.dt.float32
BF16 = mybir.dt.bfloat16
U32 = mybir.dt.uint32
U8 = mybir.dt.uint8
FP8X4 = mybir.dt.float8_e4m3fn_x4
ACT = mybir.ActivationFunctionType
ALU = mybir.AluOpType

P = 128
PACK = 4
K_PASS = P * PACK

B, H1, H2 = 1024, 1024, 512
CAPS, CAP_DIM = 32, 16
NI = CAPS * CAP_DIM
LN_EPS = 1e-5

PASSES_1 = H1 // K_PASS
H2_TILES = H2 // P
NI_TILES = NI // P
CAPS_PER_TILE = P // CAP_DIM
ROW_TILES = B // P
LAST_ROW_TILE = ROW_TILES - 1
W2_VECTOR_UNITS = 96

FLOPS = 2 * B * H1 * H2 + 2 * B * H2 * NI


def tile_capsulenetwork_pa_kernel(tc, h1, W2, b2, Wp, bp, ln_g, ln_b, out):
    nc = tc.nc
    with ExitStack() as ctx:
        keep = ctx.enter_context(tc.tile_pool(name="keep", bufs=1))
        work = ctx.enter_context(tc.tile_pool(name="work", bufs=3))
        psum = ctx.enter_context(tc.psum_pool(name="psum", bufs=6))
        psum_mx = ctx.enter_context(tc.psum_pool(name="psum_mx", bufs=2))

        w2_raw = keep.tile([P, PASSES_1, PACK, H2], BF16)
        h1_raw = keep.tile([P, ROW_TILES, H1], BF16)
        wp_raw = keep.tile([P, CAPS, PACK, CAP_DIM], BF16)

        def load_w2_pass(g):
            nc.sync.dma_start(
                out=w2_raw[:, g].rearrange("q (u e) w -> q u (e w)", e=2),
                in_=W2[g * K_PASS : (g + 1) * K_PASS, :].rearrange("(u q e) w -> q u (e w)", u=2, e=2),
            )

        def load_h1_tile(j):
            nc.sync.dma_start(out=h1_raw[:, j, :], in_=h1[j * P : (j + 1) * P, :])

        load_w2_pass(0)
        load_h1_tile(0)
        load_w2_pass(1)
        for j in range(1, ROW_TILES):
            load_h1_tile(j)
        nc.sync.dma_start(
            out=wp_raw[:].rearrange("p n t i -> p n (t i)"),
            in_=Wp.rearrange("n (p t) i -> p n (t i)", t=PACK),
        )
        gain = keep.tile([P, NI], BF16)
        nc.sync.dma_start(out=gain[:], in_=ln_g.rearrange("n i -> (n i)").partition_broadcast(P))
        shift = keep.tile([P, NI], BF16)
        nc.sync.dma_start(out=shift[:], in_=ln_b.rearrange("n i -> (n i)").partition_broadcast(P))

        b2_bf = keep.tile([P, H2_TILES], BF16)
        nc.scalar.dma_start(out=b2_bf[:], in_=b2.rearrange("(m t) -> m t", t=H2_TILES))
        bp_rows = keep.tile([P, P], BF16)
        nc.vector.memset(bp_rows[:], 0.0)
        nc.scalar.dma_start(out=bp_rows[0:NI_TILES, :], in_=bp.rearrange("(r n) i -> r (n i)", r=NI_TILES))

        eps = keep.tile([P, 1], F32)
        nc.vector.memset(eps[:], LN_EPS)
        first_rsqrt = keep.tile([P, 1], F32)
        nc.scalar.activation(out=first_rsqrt[:], in_=eps[:], func=ACT.Abs_reciprocal_sqrt)

        ident = keep.tile([P, P], F32)
        make_identity(nc, ident[:])
        in_capsule = keep.tile([P, CAPS_PER_TILE], F32)
        nc.vector.tensor_reduce(
            out=in_capsule[:],
            in_=ident[:].rearrange("p (n i) -> p n i", i=CAP_DIM),
            axis=mybir.AxisListType.X,
            op=ALU.add,
        )
        centre = keep.tile([P, P], F32)
        nc.vector.scalar_tensor_tensor(
            out=centre[:].rearrange("p (n i) -> p n i", i=CAP_DIM),
            in0=in_capsule[:].unsqueeze(2).to_broadcast([P, CAPS_PER_TILE, CAP_DIM]),
            scalar=-1.0 / CAP_DIM,
            in1=ident[:].rearrange("p (n i) -> p n i", i=CAP_DIM),
            op0=ALU.mult,
            op1=ALU.add,
        )

        b2_col = keep.tile([P, H2_TILES], F32)
        nc.vector.tensor_copy(out=b2_col[:], in_=b2_bf[:])

        w2_grouped = keep.tile([P, PASSES_1, H2, PACK], BF16, align_bytes=64)
        w2_codes = keep.tile([P, PASSES_1, H2], U32, align_bytes=64)
        w2_scales = keep.tile([P, PASSES_1, H2], U8, align_bytes=64)
        for g in range(PASSES_1):
            grouped = w2_grouped[:, g].rearrange("p (t m) j -> p t m j", t=H2_TILES)
            raw = w2_raw[:, g].rearrange("p j (m t) -> p t m j", t=H2_TILES)
            nc.vector.tensor_copy(out=grouped[:, :, 0:W2_VECTOR_UNITS, :], in_=raw[:, :, 0:W2_VECTOR_UNITS, :])
            nc.scalar.copy(out=grouped[:, :, W2_VECTOR_UNITS:P, :], in_=raw[:, :, W2_VECTOR_UNITS:P, :])
        for g in range(PASSES_1):
            nc.vector.quantize_mx(
                out=w2_codes[:, g, :].bitcast(FP8X4),
                scales=w2_scales[:, g, :],
                in_=w2_grouped[:, g].rearrange("p c j -> p (c j)"),
            )

        wp_grouped = keep.tile([P, CAPS, CAP_DIM, PACK], BF16, align_bytes=64)
        wp_codes = keep.tile([P, NI], U32, align_bytes=64)
        wp_scales = keep.tile([P, NI], U8, align_bytes=64)

        def quantise_wp():
            nc.vector.tensor_copy(out=wp_grouped[:], in_=wp_raw[:].rearrange("p n t i -> p n i t"))
            nc.vector.quantize_mx(
                out=wp_codes[:].bitcast(FP8X4),
                scales=wp_scales[:],
                in_=wp_grouped[:].rearrange("p n i t -> p (n i t)"),
            )

        h1_words = h1_raw[:].bitcast(F32)
        h1_grouped = keep.tile([P, ROW_TILES, PASSES_1, P, PACK], BF16, align_bytes=64)
        h1_grouped_words = h1_grouped[:].bitcast(F32)
        h1_codes = keep.tile([P, ROW_TILES, PASSES_1, P], U32, align_bytes=64)
        h1_scales = keep.tile([P, ROW_TILES, PASSES_1, P], U8, align_bytes=64)
        x_tiles = keep.tile([P, H2_TILES, B], BF16)
        x_grouped = keep.tile([P, B, PACK], BF16, align_bytes=64)
        x_codes = keep.tile([P, B], U32, align_bytes=64)
        x_scales = keep.tile([P, B], U8, align_bytes=64)
        u_t = keep.tile([P, NI_TILES, B], F32)
        out_tiles = out.rearrange("(j p) n i -> j p (n i)", p=P)

        def quantise_h1(j):
            turned = psum.tile([P, PASSES_1 * 2, P], F32, tag="plain")
            for gu in range(PASSES_1 * 2):
                nc.tensor.transpose(turned[:, gu, :], h1_words[:, j, gu * P : (gu + 1) * P], ident[:])
            nc.scalar.copy(out=h1_grouped_words[:, j], in_=turned[:].rearrange("p (g u) b -> p g b u", u=2))
            nc.vector.quantize_mx(
                out=h1_codes[:, j].rearrange("p g b -> p (g b)").bitcast(FP8X4),
                scales=h1_scales[:, j].rearrange("p g b -> p (g b)"),
                in_=h1_grouped[:, j].rearrange("p g b t -> p (g b t)"),
            )

        def first_product(j):
            rows = slice(j * P, (j + 1) * P)
            acc = psum_mx.tile([P, H2_TILES, P], F32, tag="mx")
            for t in range(H2_TILES):
                units = slice(t * P, (t + 1) * P)
                for g in range(PASSES_1):
                    nc.tensor.matmul_mx(
                        out=acc[:, t, :],
                        lhsT=w2_codes[:, g, units].bitcast(FP8X4),
                        lhsT_scale=w2_scales[:, g, units],
                        rhs=h1_codes[:, j, g, :].bitcast(FP8X4),
                        rhs_scale=h1_scales[:, j, g, :],
                        start=(g == 0),
                        stop=(g == PASSES_1 - 1),
                    )
            for t in range(H2_TILES):
                nc.scalar.activation(
                    out=x_tiles[:, t, rows], in_=acc[:, t, :], func=ACT.Relu, bias=b2_col[:, t : t + 1], scale=1.0
                )
            nc.vector.tensor_copy(
                out=x_grouped[:, rows, :].rearrange("p (c i) t -> p c t i", i=4),
                in_=x_tiles[:, :, rows].rearrange("p t (c i) -> p c t i", i=4),
            )
            nc.vector.quantize_mx(
                out=x_codes[:, rows].bitcast(FP8X4),
                scales=x_scales[:, rows],
                in_=x_grouped[:, rows, :].rearrange("p b t -> p (b t)"),
            )

        def second_product(j):
            rows = slice(j * P, (j + 1) * P)
            acc_t = psum_mx.tile([P, NI_TILES, P], F32, tag="mx")
            for r in range(NI_TILES):
                cols = slice(r * P, (r + 1) * P)
                nc.tensor.matmul_mx(
                    out=acc_t[:, r, :],
                    lhsT=wp_codes[:, cols].bitcast(FP8X4),
                    lhsT_scale=wp_scales[:, cols],
                    rhs=x_codes[:, rows].bitcast(FP8X4),
                    rhs_scale=x_scales[:, rows],
                    start=True,
                    stop=True,
                )
            for r in range(NI_TILES):
                nc.scalar.activation(
                    out=u_t[:, r, rows], in_=acc_t[:, r, :], func=ACT.Identity, bias=bp_col[:, r : r + 1], scale=1.0
                )

        def layer_norm(j):
            rows = slice(j * P, (j + 1) * P)
            centred = psum.tile([P, NI], F32, tag="plain")
            for r in range(NI_TILES):
                nc.tensor.matmul(
                    out=centred[:, r * P : (r + 1) * P], lhsT=u_t[:, r, rows], rhs=centre[:], start=True, stop=True
                )
            squares = work.tile([P, NI], F32)
            nc.scalar.activation(out=squares[:], in_=centred[:], func=ACT.Square)
            sum_sq = work.tile([P, CAPS], F32)
            nc.vector.tensor_reduce(
                out=sum_sq[:],
                in_=squares[:].rearrange("p (n i) -> p n i", i=CAP_DIM),
                axis=mybir.AxisListType.X,
                op=ALU.add,
            )
            rstd = work.tile([P, CAPS], F32)
            nc.scalar.activation(
                out=rstd[:], in_=sum_sq[:], func=ACT.Abs_reciprocal_sqrt, bias=eps[:, 0:1], scale=1.0 / CAP_DIM
            )
            factor = work.tile([P, NI], F32)
            factor_engine = nc.vector if j == LAST_ROW_TILE else nc.gpsimd
            factor_engine.tensor_tensor(
                out=factor[:].rearrange("p (n i) -> p n i", i=CAP_DIM),
                in0=gain[:].rearrange("p (n i) -> p n i", i=CAP_DIM),
                in1=rstd[:].unsqueeze(2).to_broadcast([P, CAPS, CAP_DIM]),
                op=ALU.mult,
            )
            scaled = work.tile([P, NI], F32)
            nc.vector.tensor_tensor(out=scaled[:], in0=centred[:], in1=factor[:], op=ALU.mult)
            result = work.tile([P, NI], F32)
            nc.vector.tensor_tensor(out=result[:], in0=scaled[:], in1=shift[:], op=ALU.add)
            nc.sync.dma_start(out=out_tiles[j], in_=result[:])

        for j in range(ROW_TILES):
            quantise_h1(j)
        quantise_wp()
        for j in range(ROW_TILES):
            first_product(j)

        bp_rows_f = keep.tile([P, P], F32)
        nc.vector.tensor_copy(out=bp_rows_f[:], in_=bp_rows[:])
        bp_ps = psum.tile([P, P], F32, tag="plain")
        nc.tensor.transpose(bp_ps[:], bp_rows_f[:], ident[:])
        bp_col = keep.tile([P, NI_TILES], F32)
        nc.vector.tensor_copy(out=bp_col[:], in_=bp_ps[:, 0:NI_TILES])

        second_product(0)
        for j in range(ROW_TILES):
            if j + 1 < ROW_TILES:
                second_product(j + 1)
            layer_norm(j)
